import numpy as np
import ml_dtypes


def mxq(x, axis, fmt="e4m3"):
    dtype, down = {"e4m3": (ml_dtypes.float8_e4m3fn, 7), "e5m2": (ml_dtypes.float8_e5m2, 14)}[fmt]
    v = np.moveaxis(np.asarray(x, np.float32).astype(ml_dtypes.bfloat16).astype(np.float64), axis, -1)
    blocks = v.reshape(v.shape[:-1] + (-1, 32))
    amax = np.abs(blocks).max(-1, keepdims=True)
    byte = np.maximum(np.where(amax > 0, np.frexp(amax)[1] - 1 + 127, 0) - down, 1)
    scale = np.exp2(byte - 127.0)
    codes = (blocks / scale).astype(np.float32).astype(dtype).astype(np.float64)
    return np.moveaxis((codes * scale).reshape(v.shape), -1, axis)


WIDE = False


def mx_kscale(k):
    if not WIDE:
        return np.ones(k)
    levels = np.array([10, -10, 5, -5, 0])
    a = np.random.permutation(np.resize(levels, k // 512 * 4)).reshape(k // 512, 4)
    idx = np.arange(k)
    return np.exp2(a[idx // 512, idx % 128 // 32])


BF16 = ml_dtypes.bfloat16


def bf(x):
    return np.asarray(x, np.float32).astype(BF16)


def f64(x):
    return np.asarray(x).astype(np.float64)


B, Q, S, D = 4, 256, 512, 1024
K = D + D


def sigmoid(v):
    return 1.0 / (1.0 + np.exp(-v))


def setup_inputs():
    t = mx_kscale(D)
    s = np.concatenate([np.ones(D), t])
    return {"query": bf(np.random.standard_normal((B, Q, D)) * 0.25),
            "weighted_ctx": bf(np.random.standard_normal((B, Q, D)) * 0.12 * t),
            "W_lin": bf(np.random.standard_normal((K, D)) * 5.0 / np.sqrt(K) / s[:, None]),
            "b_lin": bf(np.random.standard_normal(D) * 0.3),
            "W_gate": bf(np.random.standard_normal((K, D)) * 5.0 / np.sqrt(K) / s[:, None]),
            "b_gate": bf(np.random.standard_normal(D) * 0.3)}


def reference(query, weighted_ctx, W_lin, b_lin, W_gate, b_gate):
    q = f64(query)
    cat = mxq(np.concatenate([q, f64(weighted_ctx)], axis=2), 2, "e4m3")
    h = np.tanh((cat @ mxq(f64(W_lin), 0, "e4m3")) + f64(b_lin))
    g = sigmoid((cat @ mxq(f64(W_gate), 0, "e4m3")) + f64(b_gate))
    return q * g + h * (1.0 - g)

@@ -1,0 +1,229 @@
+from contextlib import ExitStack
+
+import concourse.masks as masks
+import concourse.mybir as mybir
+
+FP8X4 = mybir.dt.float8_e4m3fn_x4
+BF16 = mybir.dt.bfloat16
+F32 = mybir.dt.float32
+U32 = mybir.dt.uint32
+U8 = mybir.dt.uint8
+ACT = mybir.ActivationFunctionType
+ALU = mybir.AluOpType
+
+P = 128
+PACK = 4
+K_PASS = P * PACK
+TOKENS = 1024
+FEATURES = 1024
+PASSES = 2 * FEATURES // K_PASS
+QUERY_PASSES = FEATURES // K_PASS
+TOKEN_TILES = TOKENS // P
+HALF = 512
+HALVES = TOKENS // HALF
+TILES_PER_HALF = HALF // P
+BLOCK = 256
+BLOCKS = FEATURES // BLOCK
+SLICES = BLOCK // P
+SCALAR_PASSES = 2
+
+FLOPS = 2 * TOKENS * 2 * FEATURES * 2 * FEATURES
+
+
+def tile_smcmr_pb_kernel(tc, query, weighted_ctx, W_lin, b_lin, W_gate, b_gate, out):
+    nc = tc.nc
+    q_dram = query.flatten_outer_dims().rearrange("(p i) d -> p i d", i=TOKEN_TILES)
+    c_dram = weighted_ctx.flatten_outer_dims().rearrange("(p i) d -> p i d", i=TOKEN_TILES)
+    out_dram = out.flatten_outer_dims().rearrange("(p i) d -> p i d", i=TOKEN_TILES)
+
+    with ExitStack() as ctx:
+        keep = ctx.enter_context(tc.tile_pool(name="keep", bufs=1))
+        raw_pool = ctx.enter_context(tc.tile_pool(name="raw", bufs=1))
+        grouped_pool = ctx.enter_context(tc.tile_pool(name="grouped", bufs=4))
+        weight_pool = ctx.enter_context(tc.tile_pool(name="weights", bufs=3))
+        hidden_pool = ctx.enter_context(tc.tile_pool(name="hidden", bufs=8))
+        gate_pool = ctx.enter_context(tc.tile_pool(name="gate", bufs=6))
+        result_pool = ctx.enter_context(tc.tile_pool(name="result", bufs=4))
+        acc_pool = ctx.enter_context(tc.psum_pool(name="acc", bufs=4))
+        flip_pool = ctx.enter_context(tc.psum_pool(name="flip", bufs=4))
+
+        ident_bf16 = keep.tile([P, P], BF16)
+        masks.make_identity(nc, ident_bf16[:])
+        ident_f32 = keep.tile([P, P], F32)
+        masks.make_identity(nc, ident_f32[:])
+
+        warm_in = keep.tile([P, 1], F32)
+        warm_out = keep.tile([P, 1], F32)
+        nc.vector.memset(warm_in[:], 0.0)
+        nc.scalar.activation(out=warm_out[:], in_=warm_in[:], func=ACT.Sigmoid)
+
+        bias_rows = keep.tile([P, P], BF16)
+        nc.vector.memset(bias_rows[:], 0.0)
+        nc.scalar.dma_start(out=bias_rows[0:8, :], in_=b_lin.rearrange("(s j) -> s j", j=P))
+        nc.scalar.dma_start(out=bias_rows[8:16, :], in_=b_gate.rearrange("(s j) -> s j", j=P))
+
+        q_sb = keep.tile([P, TOKEN_TILES, FEATURES], BF16)
+        c_sb = keep.tile([P, TOKEN_TILES * FEATURES], BF16)
+        c_tiles = c_sb[:].rearrange("p (i d) -> p i d", i=TOKEN_TILES)
+        c_words = c_sb[:].bitcast(F32)
+
+        def load_tokens(half):
+            tiles = slice(half * TILES_PER_HALF, (half + 1) * TILES_PER_HALF)
+            nc.sync.dma_start(out=q_sb[:, tiles, :], in_=q_dram[:, tiles, :])
+            nc.sync.dma_start(out=c_tiles[:, tiles, :], in_=c_dram[:, tiles, :])
+
+        def load_weights(w, block, name):
+            cols = slice(block * BLOCK, (block + 1) * BLOCK)
+            raw = raw_pool.tile([P, PASSES * PACK, BLOCK], BF16, name=name)
+            nc.sync.dma_start(
+                out=raw[:, 0 : QUERY_PASSES * PACK, :],
+                in_=w[0:FEATURES, cols].rearrange("(r p) n -> p r n", p=P),
+            )
+            pairs = w[FEATURES : 2 * FEATURES, cols].rearrange("(v p e) n -> e p v n", p=P, e=2)
+            for e in range(2):
+                nc.sync.dma_start(out=raw[:, QUERY_PASSES * PACK + e : PASSES * PACK : 2, :], in_=pairs[e])
+            return raw
+
+        raws = []
+        raws.append(load_weights(W_lin, 0, "raw_lin0"))
+        load_tokens(0)
+        raws.append(load_weights(W_gate, 0, "raw_gate0"))
+        load_tokens(1)
+        for block in range(1, BLOCKS):
+            raws.append(load_weights(W_lin, block, "raw_lin%d" % block))
+            raws.append(load_weights(W_gate, block, "raw_gate%d" % block))
+
+        grouped_q = keep.tile([P, QUERY_PASSES * TOKENS * PACK], BF16, align_bytes=64)
+        grouped_q4 = grouped_q[:].rearrange("p (g r t) -> p g r t", g=QUERY_PASSES, t=PACK)
+        grouped_c = keep.tile([P, QUERY_PASSES * TOKENS * PACK], BF16, align_bytes=64)
+        grouped_c_words = grouped_c[:].bitcast(F32).rearrange("p (g r u) -> p g r u", g=QUERY_PASSES, u=2)
+        cat_codes = keep.tile([P, PASSES, TOKENS], U32, align_bytes=64)
+        cat_scales = keep.tile([P, PASSES, TOKENS], U8, align_bytes=64)
+
+        def prepare_tokens(half):
+            first = half * TILES_PER_HALF
+            for i in range(first, first + TILES_PER_HALF):
+                for g in range(QUERY_PASSES):
+                    flipped_q = flip_pool.tile([P, PACK, P], BF16, tag="flip")
+                    for t in range(PACK):
+                        k0 = g * K_PASS + t * P
+                        nc.tensor.transpose(flipped_q[:, t, :], q_sb[:, i, k0 : k0 + P], ident_bf16[:])
+                    nc.scalar.copy(
+                        out=grouped_q4[:, g, i * P : (i + 1) * P, :],
+                        in_=flipped_q[:].rearrange("p t r -> p r t"),
+                    )
+            for g in range(QUERY_PASSES):
+                start = (g * TOKENS + half * HALF) * PACK
+                nc.vector.quantize_mx(
+                    out=cat_codes[:, g, half * HALF : (half + 1) * HALF].bitcast(FP8X4),
+                    scales=cat_scales[:, g, half * HALF : (half + 1) * HALF],
+                    in_=grouped_q[:, start : start + HALF * PACK],
+                )
+            for i in range(first, first + TILES_PER_HALF, 2):
+                for g in range(QUERY_PASSES):
+                    flipped_c = flip_pool.tile([P, 2, 2, P], F32, tag="flip")
+                    for a in range(2):
+                        for u in range(2):
+                            w0 = (i + a) * (FEATURES // 2) + g * (K_PASS // 2) + u * P
+                            nc.tensor.transpose(flipped_c[:, a, u, :], c_words[:, w0 : w0 + P], ident_f32[:])
+                    nc.vector.tensor_copy(
+                        out=grouped_c_words[:, g, i * P : (i + 2) * P, :].rearrange("p (a r) u -> p a r u", a=2),
+                        in_=flipped_c[:].rearrange("p a u r -> p a r u"),
+                    )
+            for g in range(QUERY_PASSES):
+                start = (g * TOKENS + half * HALF) * PACK
+                c = QUERY_PASSES + g
+                nc.vector.quantize_mx(
+                    out=cat_codes[:, c, half * HALF : (half + 1) * HALF].bitcast(FP8X4),
+                    scales=cat_scales[:, c, half * HALF : (half + 1) * HALF],
+                    in_=grouped_c[:, start : start + HALF * PACK],
+                )
+
+        def prepare_weights(raw):
+            codes = weight_pool.tile([P, PASSES, BLOCK], U32, align_bytes=64, tag="codes")
+            scales = weight_pool.tile([P, PASSES, BLOCK], U8, align_bytes=64, tag="scales")
+            for first in range(0, PASSES, 2):
+                grouped_w = grouped_pool.tile([P, 2, BLOCK, PACK], BF16, align_bytes=64, tag="grouped_w")
+                for c in range(first, first + 2):
+                    dst = grouped_w[:, c - first].rearrange("p (a i) t -> p a t i", i=4)
+                    src = raw[:, c * PACK : (c + 1) * PACK, :].rearrange("p t (a i) -> p a t i", i=4)
+                    if c < SCALAR_PASSES:
+                        nc.scalar.copy(out=dst, in_=src)
+                    else:
+                        nc.vector.tensor_copy(out=dst, in_=src)
+                nc.vector.quantize_mx(
+                    out=codes[:, first : first + 2, :].rearrange("p c n -> p (c n)").bitcast(FP8X4),
+                    scales=scales[:, first : first + 2, :].rearrange("p c n -> p (c n)"),
+                    in_=grouped_w[:].rearrange("p c n t -> p (c n t)"),
+                )
+            return codes, scales
+
+        def multiply(weights, s, half):
+            codes, scales = weights
+            feats = slice(s * P, (s + 1) * P)
+            toks = slice(half * HALF, (half + 1) * HALF)
+            acc = acc_pool.tile([P, HALF], F32, tag="acc")
+            for c in range(PASSES):
+                nc.tensor.matmul_mx(
+                    out=acc[:],
+                    lhsT=codes[:, c, feats].bitcast(FP8X4),
+                    lhsT_scale=scales[:, c, feats],
+                    rhs=cat_codes[:, c, toks].bitcast(FP8X4),
+                    rhs_scale=cat_scales[:, c, toks],
+                    start=(c == 0),
+                    stop=(c == PASSES - 1),
+                )
+            return acc
+
+        ready = [prepare_weights(raws[0])]
+        prepare_tokens(0)
+
+        bias_cols = flip_pool.tile([P, P], BF16, tag="flip")
+        nc.tensor.transpose(bias_cols[:], bias_rows[:], ident_bf16[:])
+        bias_lin = keep.tile([P, 8], F32)
+        nc.vector.tensor_copy(out=bias_lin[:], in_=bias_cols[:, 0:8])
+        neg_bias_gate = keep.tile([P, 8], F32)
+        nc.vector.tensor_scalar_mul(out=neg_bias_gate[:], in0=bias_cols[:, 8:16], scalar1=-1.0)
+
+        ready.append(prepare_weights(raws[1]))
+        prepare_tokens(1)
+
+        for block in range(BLOCKS):
+            mixes = {}
+            for half in range(HALVES):
+                for s in range(SLICES):
+                    n = block * SLICES + s
+                    acc_lin = multiply(ready[2 * block], s, half)
+                    mix = hidden_pool.tile([P, HALF], F32, tag="mix")
+                    nc.scalar.activation(out=mix[:], in_=acc_lin[:], func=ACT.Tanh, bias=bias_lin[:, n : n + 1], scale=1.0)
+                    q_t = grouped_q4[:, n // PACK, half * HALF : (half + 1) * HALF, n % PACK]
+                    nc.vector.tensor_sub(out=mix[:], in0=mix[:], in1=q_t)
+                    mixes[(half, s)] = mix
+            if block + 1 < BLOCKS:
+                ready.append(prepare_weights(raws[2 * block + 2]))
+            for half in range(HALVES):
+                for s in range(SLICES):
+                    n = block * SLICES + s
+                    acc_gate = multiply(ready[2 * block + 1], s, half)
+                    away = gate_pool.tile([P, HALF], F32, tag="away")
+                    nc.scalar.activation(
+                        out=away[:], in_=acc_gate[:], func=ACT.Sigmoid, bias=neg_bias_gate[:, n : n + 1], scale=-1.0
+                    )
+                    mix = mixes[(half, s)]
+                    nc.vector.tensor_mul(out=mix[:], in0=mix[:], in1=away[:])
+            if block + 1 < BLOCKS:
+                ready.append(prepare_weights(raws[2 * block + 3]))
+            for half in range(HALVES):
+                for pair in range(TILES_PER_HALF // 2):
+                    back = flip_pool.tile([P, 2, SLICES, P], F32, tag="flip")
+                    for a in range(2):
+                        for s in range(SLICES):
+                            r0 = (2 * pair + a) * P
+                            nc.tensor.transpose(back[:, a, s, :], mixes[(half, s)][:, r0 : r0 + P], ident_f32[:])
+                    i0 = half * TILES_PER_HALF + 2 * pair
+                    cols = slice(block * BLOCK, (block + 1) * BLOCK)
+                    result = result_pool.tile([P, 2, BLOCK], F32, tag="result")
+                    nc.vector.tensor_add(
+                        out=result[:], in0=back[:].rearrange("p a s j -> p a (s j)"), in1=q_sb[:, i0 : i0 + 2, cols]
+                    )
+                    nc.sync.dma_start(out=out_dram[:, i0 : i0 + 2, cols], in_=result[:])

@@ -25,7 +25,8 @@ TILES_PER_HALF = HALF // P
 BLOCK = 256
 BLOCKS = FEATURES // BLOCK
 SLICES = BLOCK // P
-SCALAR_PASSES = 2
+STEPS = 2 * BLOCKS
+SCALAR_PASSES = 3
 
 FLOPS = 2 * TOKENS * 2 * FEATURES * 2 * FEATURES
 
@@ -37,9 +38,10 @@ def tile_smcmr_pb_kernel(tc, query, weighted_ctx, W_lin, b_lin, W_gate, b_gate, 
     out_dram = out.flatten_outer_dims().rearrange("(p i) d -> p i d", i=TOKEN_TILES)
 
     with ExitStack() as ctx:
+        ctx.enter_context(tc.manual_schedule())
         keep = ctx.enter_context(tc.tile_pool(name="keep", bufs=1))
         raw_pool = ctx.enter_context(tc.tile_pool(name="raw", bufs=1))
-        grouped_pool = ctx.enter_context(tc.tile_pool(name="grouped", bufs=4))
+        grouped_pool = ctx.enter_context(tc.tile_pool(name="grouped", bufs=2))
         weight_pool = ctx.enter_context(tc.tile_pool(name="weights", bufs=3))
         hidden_pool = ctx.enter_context(tc.tile_pool(name="hidden", bufs=8))
         gate_pool = ctx.enter_context(tc.tile_pool(name="gate", bufs=6))
@@ -87,8 +89,8 @@ def tile_smcmr_pb_kernel(tc, query, weighted_ctx, W_lin, b_lin, W_gate, b_gate, 
         raws = []
         raws.append(load_weights(W_lin, 0, "raw_lin0"))
         load_tokens(0)
-        raws.append(load_weights(W_gate, 0, "raw_gate0"))
         load_tokens(1)
+        raws.append(load_weights(W_gate, 0, "raw_gate0"))
         for block in range(1, BLOCKS):
             raws.append(load_weights(W_lin, block, "raw_lin%d" % block))
             raws.append(load_weights(W_gate, block, "raw_gate%d" % block))
@@ -100,6 +102,14 @@ def tile_smcmr_pb_kernel(tc, query, weighted_ctx, W_lin, b_lin, W_gate, b_gate, 
         cat_codes = keep.tile([P, PASSES, TOKENS], U32, align_bytes=64)
         cat_scales = keep.tile([P, PASSES, TOKENS], U8, align_bytes=64)
 
+        def quantise_tokens(grouped, g, c, half):
+            start = (g * TOKENS + half * HALF) * PACK
+            nc.vector.quantize_mx(
+                out=cat_codes[:, c, half * HALF : (half + 1) * HALF].bitcast(FP8X4),
+                scales=cat_scales[:, c, half * HALF : (half + 1) * HALF],
+                in_=grouped[:, start : start + HALF * PACK],
+            )
+
         def prepare_tokens(half):
             first = half * TILES_PER_HALF
             for i in range(first, first + TILES_PER_HALF):
@@ -108,17 +118,14 @@ def tile_smcmr_pb_kernel(tc, query, weighted_ctx, W_lin, b_lin, W_gate, b_gate, 
                     for t in range(PACK):
                         k0 = g * K_PASS + t * P
                         nc.tensor.transpose(flipped_q[:, t, :], q_sb[:, i, k0 : k0 + P], ident_bf16[:])
-                    nc.scalar.copy(
-                        out=grouped_q4[:, g, i * P : (i + 1) * P, :],
-                        in_=flipped_q[:].rearrange("p t r -> p r t"),
-                    )
+                    dst = grouped_q4[:, g, i * P : (i + 1) * P, :]
+                    src = flipped_q[:].rearrange("p t r -> p r t")
+                    if g == 0:
+                        nc.scalar.copy(out=dst, in_=src)
+                    else:
+                        nc.vector.tensor_copy(out=dst, in_=src)
             for g in range(QUERY_PASSES):
-                start = (g * TOKENS + half * HALF) * PACK
-                nc.vector.quantize_mx(
-                    out=cat_codes[:, g, half * HALF : (half + 1) * HALF].bitcast(FP8X4),
-                    scales=cat_scales[:, g, half * HALF : (half + 1) * HALF],
-                    in_=grouped_q[:, start : start + HALF * PACK],
-                )
+                quantise_tokens(grouped_q, g, g, half)
             for i in range(first, first + TILES_PER_HALF, 2):
                 for g in range(QUERY_PASSES):
                     flipped_c = flip_pool.tile([P, 2, 2, P], F32, tag="flip")
@@ -126,35 +133,32 @@ def tile_smcmr_pb_kernel(tc, query, weighted_ctx, W_lin, b_lin, W_gate, b_gate, 
                         for u in range(2):
                             w0 = (i + a) * (FEATURES // 2) + g * (K_PASS // 2) + u * P
                             nc.tensor.transpose(flipped_c[:, a, u, :], c_words[:, w0 : w0 + P], ident_f32[:])
-                    nc.vector.tensor_copy(
+                    nc.scalar.copy(
                         out=grouped_c_words[:, g, i * P : (i + 2) * P, :].rearrange("p (a r) u -> p a r u", a=2),
                         in_=flipped_c[:].rearrange("p a u r -> p a r u"),
                     )
             for g in range(QUERY_PASSES):
-                start = (g * TOKENS + half * HALF) * PACK
-                c = QUERY_PASSES + g
-                nc.vector.quantize_mx(
-                    out=cat_codes[:, c, half * HALF : (half + 1) * HALF].bitcast(FP8X4),
-                    scales=cat_scales[:, c, half * HALF : (half + 1) * HALF],
-                    in_=grouped_c[:, start : start + HALF * PACK],
-                )
+                quantise_tokens(grouped_c, g, QUERY_PASSES + g, half)
 
-        def prepare_weights(raw):
+        def regroup_weights(raw):
+            grouped_w = grouped_pool.tile([P, PASSES, BLOCK, PACK], BF16, align_bytes=64, tag="grouped_w")
+            for c in range(PASSES):
+                dst = grouped_w[:, c].rearrange("p (a i) t -> p a t i", i=4)
+                src = raw[:, c * PACK : (c + 1) * PACK, :].rearrange("p t (a i) -> p a t i", i=4)
+                if c < SCALAR_PASSES:
+                    nc.scalar.copy(out=dst, in_=src)
+                else:
+                    nc.vector.tensor_copy(out=dst, in_=src)
+            return grouped_w
+
+        def quantise_weights(grouped_w):
             codes = weight_pool.tile([P, PASSES, BLOCK], U32, align_bytes=64, tag="codes")
             scales = weight_pool.tile([P, PASSES, BLOCK], U8, align_bytes=64, tag="scales")
             for first in range(0, PASSES, 2):
-                grouped_w = grouped_pool.tile([P, 2, BLOCK, PACK], BF16, align_bytes=64, tag="grouped_w")
-                for c in range(first, first + 2):
-                    dst = grouped_w[:, c - first].rearrange("p (a i) t -> p a t i", i=4)
-                    src = raw[:, c * PACK : (c + 1) * PACK, :].rearrange("p t (a i) -> p a t i", i=4)
-                    if c < SCALAR_PASSES:
-                        nc.scalar.copy(out=dst, in_=src)
-                    else:
-                        nc.vector.tensor_copy(out=dst, in_=src)
                 nc.vector.quantize_mx(
                     out=codes[:, first : first + 2, :].rearrange("p c n -> p (c n)").bitcast(FP8X4),
                     scales=scales[:, first : first + 2, :].rearrange("p c n -> p (c n)"),
-                    in_=grouped_w[:].rearrange("p c n t -> p (c n t)"),
+                    in_=grouped_w[:, first : first + 2].rearrange("p c n t -> p (c n t)"),
                 )
             return codes, scales
 
@@ -175,7 +179,63 @@ def tile_smcmr_pb_kernel(tc, query, weighted_ctx, W_lin, b_lin, W_gate, b_gate, 
                 )
             return acc
 
-        ready = [prepare_weights(raws[0])]
+        pieces = [(half, s) for half in range(HALVES) for s in range(SLICES)]
+        mixes = {}
+        aways = {}
+        backs = {}
+
+        def step(m, weights):
+            block = m // 2
+            for half, s in pieces:
+                n = block * SLICES + s
+                acc = multiply(weights, s, half)
+                if m % 2 == 0:
+                    mix = hidden_pool.tile([P, HALF], F32, tag="mix")
+                    nc.scalar.activation(out=mix[:], in_=acc[:], func=ACT.Tanh, bias=bias_lin[:, n : n + 1], scale=1.0)
+                    mixes[(block, half, s)] = mix
+                else:
+                    away = gate_pool.tile([P, HALF], F32, tag="away")
+                    nc.scalar.activation(
+                        out=away[:], in_=acc[:], func=ACT.Sigmoid, bias=neg_bias_gate[:, n : n + 1], scale=-1.0
+                    )
+                    aways[(block, half, s)] = away
+
+        def subtract_query(block):
+            for half, s in pieces:
+                n = block * SLICES + s
+                mix = mixes[(block, half, s)]
+                q_t = grouped_q4[:, n // PACK, half * HALF : (half + 1) * HALF, n % PACK]
+                nc.vector.tensor_sub(out=mix[:], in0=mix[:], in1=q_t)
+
+        def weigh(block):
+            for half, s in pieces:
+                mix = mixes[(block, half, s)]
+                nc.vector.tensor_mul(out=mix[:], in0=mix[:], in1=aways[(block, half, s)][:])
+
+        def transpose_back(block):
+            for half in range(HALVES):
+                for pair in range(TILES_PER_HALF // 2):
+                    back = flip_pool.tile([P, 2, SLICES, P], F32, tag="flip")
+                    for a in range(2):
+                        for s in range(SLICES):
+                            r0 = (2 * pair + a) * P
+                            nc.tensor.transpose(back[:, a, s, :], mixes[(block, half, s)][:, r0 : r0 + P], ident_f32[:])
+                    backs[(block, half, pair)] = back
+
+        def add_query_and_store(block):
+            cols = slice(block * BLOCK, (block + 1) * BLOCK)
+            for half in range(HALVES):
+                for pair in range(TILES_PER_HALF // 2):
+                    i0 = half * TILES_PER_HALF + 2 * pair
+                    result = result_pool.tile([P, 2, BLOCK], F32, tag="result")
+                    nc.vector.tensor_add(
+                        out=result[:],
+                        in0=backs[(block, half, pair)][:].rearrange("p a s j -> p a (s j)"),
+                        in1=q_sb[:, i0 : i0 + 2, cols],
+                    )
+                    nc.sync.dma_start(out=out_dram[:, i0 : i0 + 2, cols], in_=result[:])
+
+        weights = quantise_weights(regroup_weights(raws[0]))
         prepare_tokens(0)
 
         bias_cols = flip_pool.tile([P, P], BF16, tag="flip")
@@ -185,45 +245,19 @@ def tile_smcmr_pb_kernel(tc, query, weighted_ctx, W_lin, b_lin, W_gate, b_gate, 
         neg_bias_gate = keep.tile([P, 8], F32)
         nc.vector.tensor_scalar_mul(out=neg_bias_gate[:], in0=bias_cols[:, 8:16], scalar1=-1.0)
 
-        ready.append(prepare_weights(raws[1]))
         prepare_tokens(1)
 
-        for block in range(BLOCKS):
-            mixes = {}
-            for half in range(HALVES):
-                for s in range(SLICES):
-                    n = block * SLICES + s
-                    acc_lin = multiply(ready[2 * block], s, half)
-                    mix = hidden_pool.tile([P, HALF], F32, tag="mix")
-                    nc.scalar.activation(out=mix[:], in_=acc_lin[:], func=ACT.Tanh, bias=bias_lin[:, n : n + 1], scale=1.0)
-                    q_t = grouped_q4[:, n // PACK, half * HALF : (half + 1) * HALF, n % PACK]
-                    nc.vector.tensor_sub(out=mix[:], in0=mix[:], in1=q_t)
-                    mixes[(half, s)] = mix
-            if block + 1 < BLOCKS:
-                ready.append(prepare_weights(raws[2 * block + 2]))
-            for half in range(HALVES):
-                for s in range(SLICES):
-                    n = block * SLICES + s
-                    acc_gate = multiply(ready[2 * block + 1], s, half)
-                    away = gate_pool.tile([P, HALF], F32, tag="away")
-                    nc.scalar.activation(
-                        out=away[:], in_=acc_gate[:], func=ACT.Sigmoid, bias=neg_bias_gate[:, n : n + 1], scale=-1.0
-                    )
-                    mix = mixes[(half, s)]
-                    nc.vector.tensor_mul(out=mix[:], in0=mix[:], in1=away[:])
-            if block + 1 < BLOCKS:
-                ready.append(prepare_weights(raws[2 * block + 3]))
-            for half in range(HALVES):
-                for pair in range(TILES_PER_HALF // 2):
-                    back = flip_pool.tile([P, 2, SLICES, P], F32, tag="flip")
-                    for a in range(2):
-                        for s in range(SLICES):
-                            r0 = (2 * pair + a) * P
-                            nc.tensor.transpose(back[:, a, s, :], mixes[(half, s)][:, r0 : r0 + P], ident_f32[:])
-                    i0 = half * TILES_PER_HALF + 2 * pair
-                    cols = slice(block * BLOCK, (block + 1) * BLOCK)
-                    result = result_pool.tile([P, 2, BLOCK], F32, tag="result")
-                    nc.vector.tensor_add(
-                        out=result[:], in0=back[:].rearrange("p a s j -> p a (s j)"), in1=q_sb[:, i0 : i0 + 2, cols]
-                    )
-                    nc.sync.dma_start(out=out_dram[:, i0 : i0 + 2, cols], in_=result[:])
+        for m in range(STEPS + 2):
+            if m + 1 < STEPS:
+                grouped_next = regroup_weights(raws[m + 1])
+            if m < STEPS:
+                step(m, weights)
+            if m % 2 == 1 and m >= 3:
+                add_query_and_store((m - 3) // 2)
+            if m % 2 == 0 and m >= 2:
+                weigh((m - 2) // 2)
+                transpose_back((m - 2) // 2)
+            if m + 1 < STEPS:
+                weights = quantise_weights(grouped_next)
+            if m % 2 == 1 and m < STEPS:
+                subtract_query((m - 1) // 2)

@@ -26,7 +26,7 @@ BLOCK = 256
 BLOCKS = FEATURES // BLOCK
 SLICES = BLOCK // P
 STEPS = 2 * BLOCKS
-SCALAR_PASSES = 3
+EARLY_STEPS = 4
 
 FLOPS = 2 * TOKENS * 2 * FEATURES * 2 * FEATURES
 
@@ -43,14 +43,12 @@ def tile_smcmr_pb_kernel(tc, query, weighted_ctx, W_lin, b_lin, W_gate, b_gate, 
         raw_pool = ctx.enter_context(tc.tile_pool(name="raw", bufs=1))
         grouped_pool = ctx.enter_context(tc.tile_pool(name="grouped", bufs=2))
         weight_pool = ctx.enter_context(tc.tile_pool(name="weights", bufs=3))
-        hidden_pool = ctx.enter_context(tc.tile_pool(name="hidden", bufs=8))
-        gate_pool = ctx.enter_context(tc.tile_pool(name="gate", bufs=6))
+        hidden_pool = ctx.enter_context(tc.tile_pool(name="hidden", bufs=4))
+        gate_pool = ctx.enter_context(tc.tile_pool(name="gate", bufs=4))
         result_pool = ctx.enter_context(tc.tile_pool(name="result", bufs=4))
         acc_pool = ctx.enter_context(tc.psum_pool(name="acc", bufs=4))
         flip_pool = ctx.enter_context(tc.psum_pool(name="flip", bufs=4))
 
-        ident_bf16 = keep.tile([P, P], BF16)
-        masks.make_identity(nc, ident_bf16[:])
         ident_f32 = keep.tile([P, P], F32)
         masks.make_identity(nc, ident_f32[:])
 
@@ -59,31 +57,32 @@ def tile_smcmr_pb_kernel(tc, query, weighted_ctx, W_lin, b_lin, W_gate, b_gate, 
         nc.vector.memset(warm_in[:], 0.0)
         nc.scalar.activation(out=warm_out[:], in_=warm_in[:], func=ACT.Sigmoid)
 
-        bias_rows = keep.tile([P, P], BF16)
+        bias_rows = keep.tile([P, 2 * P], BF16)
         nc.vector.memset(bias_rows[:], 0.0)
-        nc.scalar.dma_start(out=bias_rows[0:8, :], in_=b_lin.rearrange("(s j) -> s j", j=P))
-        nc.scalar.dma_start(out=bias_rows[8:16, :], in_=b_gate.rearrange("(s j) -> s j", j=P))
+        nc.scalar.dma_start(out=bias_rows[0:BLOCKS, :], in_=b_lin.rearrange("(b n) -> b n", n=BLOCK))
+        nc.scalar.dma_start(out=bias_rows[BLOCKS : 2 * BLOCKS, :], in_=b_gate.rearrange("(b n) -> b n", n=BLOCK))
 
-        q_sb = keep.tile([P, TOKEN_TILES, FEATURES], BF16)
+        q_sb = keep.tile([P, TOKEN_TILES * FEATURES], BF16)
+        q_tiles = q_sb[:].rearrange("p (i d) -> p i d", i=TOKEN_TILES)
         c_sb = keep.tile([P, TOKEN_TILES * FEATURES], BF16)
         c_tiles = c_sb[:].rearrange("p (i d) -> p i d", i=TOKEN_TILES)
-        c_words = c_sb[:].bitcast(F32)
+        words = [q_sb[:].bitcast(F32), c_sb[:].bitcast(F32)]
 
         def load_tokens(half):
             tiles = slice(half * TILES_PER_HALF, (half + 1) * TILES_PER_HALF)
-            nc.sync.dma_start(out=q_sb[:, tiles, :], in_=q_dram[:, tiles, :])
+            nc.sync.dma_start(out=q_tiles[:, tiles, :], in_=q_dram[:, tiles, :])
             nc.sync.dma_start(out=c_tiles[:, tiles, :], in_=c_dram[:, tiles, :])
 
         def load_weights(w, block, name):
             cols = slice(block * BLOCK, (block + 1) * BLOCK)
             raw = raw_pool.tile([P, PASSES * PACK, BLOCK], BF16, name=name)
-            nc.sync.dma_start(
-                out=raw[:, 0 : QUERY_PASSES * PACK, :],
-                in_=w[0:FEATURES, cols].rearrange("(r p) n -> p r n", p=P),
-            )
-            pairs = w[FEATURES : 2 * FEATURES, cols].rearrange("(v p e) n -> e p v n", p=P, e=2)
-            for e in range(2):
-                nc.sync.dma_start(out=raw[:, QUERY_PASSES * PACK + e : PASSES * PACK : 2, :], in_=pairs[e])
+            pairs = w[:, cols].rearrange("(v p e) n -> e p v n", p=P, e=2)
+            for first in range(0, PASSES, 2):
+                for e in range(2):
+                    nc.sync.dma_start(
+                        out=raw[:, first * PACK + e : (first + 2) * PACK : 2, :],
+                        in_=pairs[e][:, first * 2 : (first + 2) * 2, :],
+                    )
             return raw
 
         raws = []
@@ -95,60 +94,49 @@ def tile_smcmr_pb_kernel(tc, query, weighted_ctx, W_lin, b_lin, W_gate, b_gate, 
             raws.append(load_weights(W_lin, block, "raw_lin%d" % block))
             raws.append(load_weights(W_gate, block, "raw_gate%d" % block))
 
-        grouped_q = keep.tile([P, QUERY_PASSES * TOKENS * PACK], BF16, align_bytes=64)
-        grouped_q4 = grouped_q[:].rearrange("p (g r t) -> p g r t", g=QUERY_PASSES, t=PACK)
-        grouped_c = keep.tile([P, QUERY_PASSES * TOKENS * PACK], BF16, align_bytes=64)
-        grouped_c_words = grouped_c[:].bitcast(F32).rearrange("p (g r u) -> p g r u", g=QUERY_PASSES, u=2)
+        grouped = keep.tile([P, PASSES * TOKENS * PACK], BF16, align_bytes=64)
+        grouped_values = grouped[:].rearrange("p (c r t) -> p c r t", c=PASSES, t=PACK)
+        grouped_words = grouped[:].bitcast(F32).rearrange("p (c r u) -> p c r u", c=PASSES, u=2)
         cat_codes = keep.tile([P, PASSES, TOKENS], U32, align_bytes=64)
         cat_scales = keep.tile([P, PASSES, TOKENS], U8, align_bytes=64)
 
-        def quantise_tokens(grouped, g, c, half):
-            start = (g * TOKENS + half * HALF) * PACK
-            nc.vector.quantize_mx(
-                out=cat_codes[:, c, half * HALF : (half + 1) * HALF].bitcast(FP8X4),
-                scales=cat_scales[:, c, half * HALF : (half + 1) * HALF],
-                in_=grouped[:, start : start + HALF * PACK],
-            )
-
         def prepare_tokens(half):
             first = half * TILES_PER_HALF
-            for i in range(first, first + TILES_PER_HALF):
+            toks = slice(half * HALF, (half + 1) * HALF)
+            for source in range(2):
+                for i in range(first, first + TILES_PER_HALF, 2):
+                    for g in range(QUERY_PASSES):
+                        c = source * QUERY_PASSES + g
+                        flipped = flip_pool.tile([P, 2, 2, P], F32, tag="flip")
+                        for a in range(2):
+                            for u in range(2):
+                                w0 = (i + a) * (FEATURES // 2) + g * (K_PASS // 2) + u * P
+                                nc.tensor.transpose(flipped[:, a, u, :], words[source][:, w0 : w0 + P], ident_f32[:])
+                        dst = grouped_words[:, c, i * P : (i + 2) * P, :].rearrange("p (a r) u -> p a r u", a=2)
+                        src = flipped[:].rearrange("p a u r -> p a r u")
+                        if g == 0:
+                            nc.scalar.copy(out=dst, in_=src)
+                        else:
+                            nc.vector.tensor_copy(out=dst, in_=src)
                 for g in range(QUERY_PASSES):
-                    flipped_q = flip_pool.tile([P, PACK, P], BF16, tag="flip")
-                    for t in range(PACK):
-                        k0 = g * K_PASS + t * P
-                        nc.tensor.transpose(flipped_q[:, t, :], q_sb[:, i, k0 : k0 + P], ident_bf16[:])
-                    dst = grouped_q4[:, g, i * P : (i + 1) * P, :]
-                    src = flipped_q[:].rearrange("p t r -> p r t")
-                    if g == 0:
+                    c = source * QUERY_PASSES + g
+                    start = (c * TOKENS + half * HALF) * PACK
+                    nc.vector.quantize_mx(
+                        out=cat_codes[:, c, toks].bitcast(FP8X4),
+                        scales=cat_scales[:, c, toks],
+                        in_=grouped[:, start : start + HALF * PACK],
+                    )
+
+        def regroup_weights(raw, scalar_passes):
+            grouped_w = grouped_pool.tile([P, PASSES, SLICES, P, PACK], BF16, align_bytes=64, tag="grouped_w")
+            for c in range(PASSES):
+                for s in range(SLICES):
+                    dst = grouped_w[:, c, s].rearrange("p (a i) t -> p a t i", i=4)
+                    src = raw[:, c * PACK : (c + 1) * PACK, s:BLOCK:2].rearrange("p t (a i) -> p a t i", i=4)
+                    if c < scalar_passes:
                         nc.scalar.copy(out=dst, in_=src)
                     else:
                         nc.vector.tensor_copy(out=dst, in_=src)
-            for g in range(QUERY_PASSES):
-                quantise_tokens(grouped_q, g, g, half)
-            for i in range(first, first + TILES_PER_HALF, 2):
-                for g in range(QUERY_PASSES):
-                    flipped_c = flip_pool.tile([P, 2, 2, P], F32, tag="flip")
-                    for a in range(2):
-                        for u in range(2):
-                            w0 = (i + a) * (FEATURES // 2) + g * (K_PASS // 2) + u * P
-                            nc.tensor.transpose(flipped_c[:, a, u, :], c_words[:, w0 : w0 + P], ident_f32[:])
-                    nc.scalar.copy(
-                        out=grouped_c_words[:, g, i * P : (i + 2) * P, :].rearrange("p (a r) u -> p a r u", a=2),
-                        in_=flipped_c[:].rearrange("p a u r -> p a r u"),
-                    )
-            for g in range(QUERY_PASSES):
-                quantise_tokens(grouped_c, g, QUERY_PASSES + g, half)
-
-        def regroup_weights(raw):
-            grouped_w = grouped_pool.tile([P, PASSES, BLOCK, PACK], BF16, align_bytes=64, tag="grouped_w")
-            for c in range(PASSES):
-                dst = grouped_w[:, c].rearrange("p (a i) t -> p a t i", i=4)
-                src = raw[:, c * PACK : (c + 1) * PACK, :].rearrange("p t (a i) -> p a t i", i=4)
-                if c < SCALAR_PASSES:
-                    nc.scalar.copy(out=dst, in_=src)
-                else:
-                    nc.vector.tensor_copy(out=dst, in_=src)
             return grouped_w
 
         def quantise_weights(grouped_w):
@@ -158,7 +146,7 @@ def tile_smcmr_pb_kernel(tc, query, weighted_ctx, W_lin, b_lin, W_gate, b_gate, 
                 nc.vector.quantize_mx(
                     out=codes[:, first : first + 2, :].rearrange("p c n -> p (c n)").bitcast(FP8X4),
                     scales=scales[:, first : first + 2, :].rearrange("p c n -> p (c n)"),
-                    in_=grouped_w[:, first : first + 2].rearrange("p c n t -> p (c n t)"),
+                    in_=grouped_w[:, first : first + 2].rearrange("p c s j t -> p (c s j t)"),
                 )
             return codes, scales
 
@@ -179,38 +167,43 @@ def tile_smcmr_pb_kernel(tc, query, weighted_ctx, W_lin, b_lin, W_gate, b_gate, 
                 )
             return acc
 
-        pieces = [(half, s) for half in range(HALVES) for s in range(SLICES)]
         mixes = {}
         aways = {}
         backs = {}
 
         def step(m, weights):
             block = m // 2
-            for half, s in pieces:
-                n = block * SLICES + s
-                acc = multiply(weights, s, half)
+            for half in range(HALVES):
                 if m % 2 == 0:
-                    mix = hidden_pool.tile([P, HALF], F32, tag="mix")
-                    nc.scalar.activation(out=mix[:], in_=acc[:], func=ACT.Tanh, bias=bias_lin[:, n : n + 1], scale=1.0)
-                    mixes[(block, half, s)] = mix
+                    value = hidden_pool.tile([P, SLICES, HALF], F32, tag="mix")
+                    mixes[(block, half)] = value
                 else:
-                    away = gate_pool.tile([P, HALF], F32, tag="away")
-                    nc.scalar.activation(
-                        out=away[:], in_=acc[:], func=ACT.Sigmoid, bias=neg_bias_gate[:, n : n + 1], scale=-1.0
-                    )
-                    aways[(block, half, s)] = away
+                    value = gate_pool.tile([P, SLICES, HALF], F32, tag="away")
+                    aways[(block, half)] = value
+                for s in range(SLICES):
+                    n = block * SLICES + s
+                    acc = multiply(weights, s, half)
+                    if m % 2 == 0:
+                        nc.scalar.activation(
+                            out=value[:, s, :], in_=acc[:], func=ACT.Tanh, bias=bias_lin[:, n : n + 1], scale=1.0
+                        )
+                    else:
+                        nc.scalar.activation(
+                            out=value[:, s, :], in_=acc[:], func=ACT.Sigmoid, bias=neg_bias_gate[:, n : n + 1], scale=-1.0
+                        )
 
         def subtract_query(block):
-            for half, s in pieces:
-                n = block * SLICES + s
-                mix = mixes[(block, half, s)]
-                q_t = grouped_q4[:, n // PACK, half * HALF : (half + 1) * HALF, n % PACK]
+            t0 = (block % 2) * SLICES
+            for half in range(HALVES):
+                mix = mixes[(block, half)]
+                toks = slice(half * HALF, (half + 1) * HALF)
+                q_t = grouped_values[:, block // 2, toks, t0 : t0 + SLICES].rearrange("p r s -> p s r")
                 nc.vector.tensor_sub(out=mix[:], in0=mix[:], in1=q_t)
 
         def weigh(block):
-            for half, s in pieces:
-                mix = mixes[(block, half, s)]
-                nc.vector.tensor_mul(out=mix[:], in0=mix[:], in1=aways[(block, half, s)][:])
+            for half in range(HALVES):
+                mix = mixes[(block, half)]
+                nc.vector.tensor_mul(out=mix[:], in0=mix[:], in1=aways[(block, half)][:])
 
         def transpose_back(block):
             for half in range(HALVES):
@@ -219,7 +212,7 @@ def tile_smcmr_pb_kernel(tc, query, weighted_ctx, W_lin, b_lin, W_gate, b_gate, 
                     for a in range(2):
                         for s in range(SLICES):
                             r0 = (2 * pair + a) * P
-                            nc.tensor.transpose(back[:, a, s, :], mixes[(block, half, s)][:, r0 : r0 + P], ident_f32[:])
+                            nc.tensor.transpose(back[:, a, s, :], mixes[(block, half)][:, s, r0 : r0 + P], ident_f32[:])
                     backs[(block, half, pair)] = back
 
         def add_query_and_store(block):
@@ -229,27 +222,31 @@ def tile_smcmr_pb_kernel(tc, query, weighted_ctx, W_lin, b_lin, W_gate, b_gate, 
                     i0 = half * TILES_PER_HALF + 2 * pair
                     result = result_pool.tile([P, 2, BLOCK], F32, tag="result")
                     nc.vector.tensor_add(
-                        out=result[:],
-                        in0=backs[(block, half, pair)][:].rearrange("p a s j -> p a (s j)"),
-                        in1=q_sb[:, i0 : i0 + 2, cols],
+                        out=result[:].rearrange("p a (j s) -> p a j s", s=SLICES),
+                        in0=backs[(block, half, pair)][:].rearrange("p a s j -> p a j s"),
+                        in1=q_tiles[:, i0 : i0 + 2, cols].rearrange("p a (j s) -> p a j s", s=SLICES),
                     )
                     nc.sync.dma_start(out=out_dram[:, i0 : i0 + 2, cols], in_=result[:])
 
-        weights = quantise_weights(regroup_weights(raws[0]))
+        def scalar_share(m):
+            return 2 if m < EARLY_STEPS else 3
+
+        weights = quantise_weights(regroup_weights(raws[0], scalar_share(0)))
         prepare_tokens(0)
 
-        bias_cols = flip_pool.tile([P, P], BF16, tag="flip")
-        nc.tensor.transpose(bias_cols[:], bias_rows[:], ident_bf16[:])
+        bias_cols = flip_pool.tile([P, P], F32, tag="flip")
+        nc.tensor.transpose(bias_cols[:], bias_rows[:].bitcast(F32), ident_f32[:])
+        bias_values = bias_cols[:].bitcast(BF16)
         bias_lin = keep.tile([P, 8], F32)
-        nc.vector.tensor_copy(out=bias_lin[:], in_=bias_cols[:, 0:8])
+        nc.vector.tensor_copy(out=bias_lin[:], in_=bias_values[:, 0:8])
         neg_bias_gate = keep.tile([P, 8], F32)
-        nc.vector.tensor_scalar_mul(out=neg_bias_gate[:], in0=bias_cols[:, 8:16], scalar1=-1.0)
+        nc.vector.tensor_scalar_mul(out=neg_bias_gate[:], in0=bias_values[:, 8:16], scalar1=-1.0)
 
         prepare_tokens(1)
 
         for m in range(STEPS + 2):
             if m + 1 < STEPS:
-                grouped_next = regroup_weights(raws[m + 1])
+                grouped_next = regroup_weights(raws[m + 1], scalar_share(m + 1))
             if m < STEPS:
                 step(m, weights)
             if m % 2 == 1 and m >= 3:

@@ -38,7 +38,6 @@ def tile_smcmr_pb_kernel(tc, query, weighted_ctx, W_lin, b_lin, W_gate, b_gate, 
     out_dram = out.flatten_outer_dims().rearrange("(p i) d -> p i d", i=TOKEN_TILES)
 
     with ExitStack() as ctx:
-        ctx.enter_context(tc.manual_schedule())
         keep = ctx.enter_context(tc.tile_pool(name="keep", bufs=1))
         raw_pool = ctx.enter_context(tc.tile_pool(name="raw", bufs=1))
         grouped_pool = ctx.enter_context(tc.tile_pool(name="grouped", bufs=2))

from contextlib import ExitStack

import concourse.masks as masks
import concourse.mybir as mybir

FP8X4 = mybir.dt.float8_e4m3fn_x4
BF16 = mybir.dt.bfloat16
F32 = mybir.dt.float32
U32 = mybir.dt.uint32
U8 = mybir.dt.uint8
ACT = mybir.ActivationFunctionType
ALU = mybir.AluOpType

P = 128
PACK = 4
K_PASS = P * PACK
TOKENS = 1024
FEATURES = 1024
PASSES = 2 * FEATURES // K_PASS
QUERY_PASSES = FEATURES // K_PASS
TOKEN_TILES = TOKENS // P
HALF = 512
HALVES = TOKENS // HALF
TILES_PER_HALF = HALF // P
BLOCK = 256
BLOCKS = FEATURES // BLOCK
SLICES = BLOCK // P
STEPS = 2 * BLOCKS
EARLY_STEPS = 4

FLOPS = 2 * TOKENS * 2 * FEATURES * 2 * FEATURES


def tile_smcmr_pb_kernel(tc, query, weighted_ctx, W_lin, b_lin, W_gate, b_gate, out):
    nc = tc.nc
    q_dram = query.flatten_outer_dims().rearrange("(p i) d -> p i d", i=TOKEN_TILES)
    c_dram = weighted_ctx.flatten_outer_dims().rearrange("(p i) d -> p i d", i=TOKEN_TILES)
    out_dram = out.flatten_outer_dims().rearrange("(p i) d -> p i d", i=TOKEN_TILES)

    with ExitStack() as ctx:
        keep = ctx.enter_context(tc.tile_pool(name="keep", bufs=1))
        raw_pool = ctx.enter_context(tc.tile_pool(name="raw", bufs=1))
        grouped_pool = ctx.enter_context(tc.tile_pool(name="grouped", bufs=2))
        weight_pool = ctx.enter_context(tc.tile_pool(name="weights", bufs=3))
        hidden_pool = ctx.enter_context(tc.tile_pool(name="hidden", bufs=4))
        gate_pool = ctx.enter_context(tc.tile_pool(name="gate", bufs=4))
        result_pool = ctx.enter_context(tc.tile_pool(name="result", bufs=4))
        acc_pool = ctx.enter_context(tc.psum_pool(name="acc", bufs=4))
        flip_pool = ctx.enter_context(tc.psum_pool(name="flip", bufs=4))

        ident_f32 = keep.tile([P, P], F32)
        masks.make_identity(nc, ident_f32[:])

        warm_in = keep.tile([P, 1], F32)
        warm_out = keep.tile([P, 1], F32)
        nc.vector.memset(warm_in[:], 0.0)
        nc.scalar.activation(out=warm_out[:], in_=warm_in[:], func=ACT.Sigmoid)

        bias_rows = keep.tile([P, 2 * P], BF16)
        nc.vector.memset(bias_rows[:], 0.0)
        nc.scalar.dma_start(out=bias_rows[0:BLOCKS, :], in_=b_lin.rearrange("(b n) -> b n", n=BLOCK))
        nc.scalar.dma_start(out=bias_rows[BLOCKS : 2 * BLOCKS, :], in_=b_gate.rearrange("(b n) -> b n", n=BLOCK))

        q_sb = keep.tile([P, TOKEN_TILES * FEATURES], BF16)
        q_tiles = q_sb[:].rearrange("p (i d) -> p i d", i=TOKEN_TILES)
        c_sb = keep.tile([P, TOKEN_TILES * FEATURES], BF16)
        c_tiles = c_sb[:].rearrange("p (i d) -> p i d", i=TOKEN_TILES)
        words = [q_sb[:].bitcast(F32), c_sb[:].bitcast(F32)]

        def load_tokens(half):
            tiles = slice(half * TILES_PER_HALF, (half + 1) * TILES_PER_HALF)
            nc.sync.dma_start(out=q_tiles[:, tiles, :], in_=q_dram[:, tiles, :])
            nc.sync.dma_start(out=c_tiles[:, tiles, :], in_=c_dram[:, tiles, :])

        def load_weights(w, block, name):
            cols = slice(block * BLOCK, (block + 1) * BLOCK)
            raw = raw_pool.tile([P, PASSES * PACK, BLOCK], BF16, name=name)
            pairs = w[:, cols].rearrange("(v p e) n -> e p v n", p=P, e=2)
            for first in range(0, PASSES, 2):
                for e in range(2):
                    nc.sync.dma_start(
                        out=raw[:, first * PACK + e : (first + 2) * PACK : 2, :],
                        in_=pairs[e][:, first * 2 : (first + 2) * 2, :],
                    )
            return raw

        raws = []
        raws.append(load_weights(W_lin, 0, "raw_lin0"))
        load_tokens(0)
        load_tokens(1)
        raws.append(load_weights(W_gate, 0, "raw_gate0"))
        for block in range(1, BLOCKS):
            raws.append(load_weights(W_lin, block, "raw_lin%d" % block))
            raws.append(load_weights(W_gate, block, "raw_gate%d" % block))

        grouped = keep.tile([P, PASSES * TOKENS * PACK], BF16, align_bytes=64)
        grouped_values = grouped[:].rearrange("p (c r t) -> p c r t", c=PASSES, t=PACK)
        grouped_words = grouped[:].bitcast(F32).rearrange("p (c r u) -> p c r u", c=PASSES, u=2)
        cat_codes = keep.tile([P, PASSES, TOKENS], U32, align_bytes=64)
        cat_scales = keep.tile([P, PASSES, TOKENS], U8, align_bytes=64)

        def prepare_tokens(half):
            first = half * TILES_PER_HALF
            toks = slice(half * HALF, (half + 1) * HALF)
            for source in range(2):
                for i in range(first, first + TILES_PER_HALF, 2):
                    for g in range(QUERY_PASSES):
                        c = source * QUERY_PASSES + g
                        flipped = flip_pool.tile([P, 2, 2, P], F32, tag="flip")
                        for a in range(2):
                            for u in range(2):
                                w0 = (i + a) * (FEATURES // 2) + g * (K_PASS // 2) + u * P
                                nc.tensor.transpose(flipped[:, a, u, :], words[source][:, w0 : w0 + P], ident_f32[:])
                        dst = grouped_words[:, c, i * P : (i + 2) * P, :].rearrange("p (a r) u -> p a r u", a=2)
                        src = flipped[:].rearrange("p a u r -> p a r u")
                        if g == 0:
                            nc.scalar.copy(out=dst, in_=src)
                        else:
                            nc.vector.tensor_copy(out=dst, in_=src)
                for g in range(QUERY_PASSES):
                    c = source * QUERY_PASSES + g
                    start = (c * TOKENS + half * HALF) * PACK
                    nc.vector.quantize_mx(
                        out=cat_codes[:, c, toks].bitcast(FP8X4),
                        scales=cat_scales[:, c, toks],
                        in_=grouped[:, start : start + HALF * PACK],
                    )

        def regroup_weights(raw, scalar_passes):
            grouped_w = grouped_pool.tile([P, PASSES, SLICES, P, PACK], BF16, align_bytes=64, tag="grouped_w")
            for c in range(PASSES):
                for s in range(SLICES):
                    dst = grouped_w[:, c, s].rearrange("p (a i) t -> p a t i", i=4)
                    src = raw[:, c * PACK : (c + 1) * PACK, s:BLOCK:2].rearrange("p t (a i) -> p a t i", i=4)
                    if c < scalar_passes:
                        nc.scalar.copy(out=dst, in_=src)
                    else:
                        nc.vector.tensor_copy(out=dst, in_=src)
            return grouped_w

        def quantise_weights(grouped_w):
            codes = weight_pool.tile([P, PASSES, BLOCK], U32, align_bytes=64, tag="codes")
            scales = weight_pool.tile([P, PASSES, BLOCK], U8, align_bytes=64, tag="scales")
            for first in range(0, PASSES, 2):
                nc.vector.quantize_mx(
                    out=codes[:, first : first + 2, :].rearrange("p c n -> p (c n)").bitcast(FP8X4),
                    scales=scales[:, first : first + 2, :].rearrange("p c n -> p (c n)"),
                    in_=grouped_w[:, first : first + 2].rearrange("p c s j t -> p (c s j t)"),
                )
            return codes, scales

        def multiply(weights, s, half):
            codes, scales = weights
            feats = slice(s * P, (s + 1) * P)
            toks = slice(half * HALF, (half + 1) * HALF)
            acc = acc_pool.tile([P, HALF], F32, tag="acc")
            for c in range(PASSES):
                nc.tensor.matmul_mx(
                    out=acc[:],
                    lhsT=codes[:, c, feats].bitcast(FP8X4),
                    lhsT_scale=scales[:, c, feats],
                    rhs=cat_codes[:, c, toks].bitcast(FP8X4),
                    rhs_scale=cat_scales[:, c, toks],
                    start=(c == 0),
                    stop=(c == PASSES - 1),
                )
            return acc

        mixes = {}
        aways = {}
        backs = {}

        def step(m, weights):
            block = m // 2
            for half in range(HALVES):
                if m % 2 == 0:
                    value = hidden_pool.tile([P, SLICES, HALF], F32, tag="mix")
                    mixes[(block, half)] = value
                else:
                    value = gate_pool.tile([P, SLICES, HALF], F32, tag="away")
                    aways[(block, half)] = value
                for s in range(SLICES):
                    n = block * SLICES + s
                    acc = multiply(weights, s, half)
                    if m % 2 == 0:
                        nc.scalar.activation(
                            out=value[:, s, :], in_=acc[:], func=ACT.Tanh, bias=bias_lin[:, n : n + 1], scale=1.0
                        )
                    else:
                        nc.scalar.activation(
                            out=value[:, s, :], in_=acc[:], func=ACT.Sigmoid, bias=neg_bias_gate[:, n : n + 1], scale=-1.0
                        )

        def subtract_query(block):
            t0 = (block % 2) * SLICES
            for half in range(HALVES):
                mix = mixes[(block, half)]
                toks = slice(half * HALF, (half + 1) * HALF)
                q_t = grouped_values[:, block // 2, toks, t0 : t0 + SLICES].rearrange("p r s -> p s r")
                nc.vector.tensor_sub(out=mix[:], in0=mix[:], in1=q_t)

        def weigh(block):
            for half in range(HALVES):
                mix = mixes[(block, half)]
                nc.vector.tensor_mul(out=mix[:], in0=mix[:], in1=aways[(block, half)][:])

        def transpose_back(block):
            for half in range(HALVES):
                for pair in range(TILES_PER_HALF // 2):
                    back = flip_pool.tile([P, 2, SLICES, P], F32, tag="flip")
                    for a in range(2):
                        for s in range(SLICES):
                            r0 = (2 * pair + a) * P
                            nc.tensor.transpose(back[:, a, s, :], mixes[(block, half)][:, s, r0 : r0 + P], ident_f32[:])
                    backs[(block, half, pair)] = back

        def add_query_and_store(block):
            cols = slice(block * BLOCK, (block + 1) * BLOCK)
            for half in range(HALVES):
                for pair in range(TILES_PER_HALF // 2):
                    i0 = half * TILES_PER_HALF + 2 * pair
                    result = result_pool.tile([P, 2, BLOCK], F32, tag="result")
                    nc.vector.tensor_add(
                        out=result[:].rearrange("p a (j s) -> p a j s", s=SLICES),
                        in0=backs[(block, half, pair)][:].rearrange("p a s j -> p a j s"),
                        in1=q_tiles[:, i0 : i0 + 2, cols].rearrange("p a (j s) -> p a j s", s=SLICES),
                    )
                    nc.sync.dma_start(out=out_dram[:, i0 : i0 + 2, cols], in_=result[:])

        def scalar_share(m):
            return 2 if m < EARLY_STEPS else 3

        weights = quantise_weights(regroup_weights(raws[0], scalar_share(0)))
        prepare_tokens(0)

        bias_cols = flip_pool.tile([P, P], F32, tag="flip")
        nc.tensor.transpose(bias_cols[:], bias_rows[:].bitcast(F32), ident_f32[:])
        bias_values = bias_cols[:].bitcast(BF16)
        bias_lin = keep.tile([P, 8], F32)
        nc.vector.tensor_copy(out=bias_lin[:], in_=bias_values[:, 0:8])
        neg_bias_gate = keep.tile([P, 8], F32)
        nc.vector.tensor_scalar_mul(out=neg_bias_gate[:], in0=bias_values[:, 8:16], scalar1=-1.0)

        prepare_tokens(1)

        for m in range(STEPS + 2):
            if m + 1 < STEPS:
                grouped_next = regroup_weights(raws[m + 1], scalar_share(m + 1))
            if m < STEPS:
                step(m, weights)
            if m % 2 == 1 and m >= 3:
                add_query_and_store((m - 3) // 2)
            if m % 2 == 0 and m >= 2:
                weigh((m - 2) // 2)
                transpose_back((m - 2) // 2)
            if m + 1 < STEPS:
                weights = quantise_weights(grouped_next)
            if m % 2 == 1 and m < STEPS:
                subtract_query((m - 1) // 2)
